import numpy as np
import ml_dtypes


def mxq(x, axis, fmt="e4m3"):
    dtype, down = {"e4m3": (ml_dtypes.float8_e4m3fn, 7), "e5m2": (ml_dtypes.float8_e5m2, 14)}[fmt]
    v = np.moveaxis(np.asarray(x, np.float32).astype(ml_dtypes.bfloat16).astype(np.float64), axis, -1)
    blocks = v.reshape(v.shape[:-1] + (-1, 32))
    amax = np.abs(blocks).max(-1, keepdims=True)
    byte = np.maximum(np.where(amax > 0, np.frexp(amax)[1] - 1 + 127, 0) - down, 1)
    scale = np.exp2(byte - 127.0)
    codes = (blocks / scale).astype(np.float32).astype(dtype).astype(np.float64)
    return np.moveaxis((codes * scale).reshape(v.shape), -1, axis)


WIDE = False


def mx_kscale(k):
    if not WIDE:
        return np.ones(k)
    levels = np.array([10, -10, 5, -5, 0])
    a = np.random.permutation(np.resize(levels, k // 512 * 4)).reshape(k // 512, 4)
    idx = np.arange(k)
    return np.exp2(a[idx // 512, idx % 128 // 32])


BF16 = ml_dtypes.bfloat16


def bf(x):
    return np.asarray(x, np.float32).astype(BF16)


def f64(x):
    return np.asarray(x).astype(np.float64)


T, D, E = 1024, 6144, 768


def setup_inputs():
    s = mx_kscale(D)
    return {"hidden_states": bf(np.random.standard_normal((T, D)) * s),
            "weight": bf(np.random.standard_normal((E, D)) * 1.0 / np.sqrt(D) / s[None, :])}


def reference(hidden_states, weight):
    logits = mxq(f64(hidden_states), 1, "e4m3") @ mxq(f64(weight), 1, "e4m3").T
    return logits

@@ -1,0 +1,262 @@
+from contextlib import ExitStack
+
+import concourse.mybir as mybir
+from concourse.masks import make_identity
+
+F32 = mybir.dt.float32
+BF16 = mybir.dt.bfloat16
+U32 = mybir.dt.uint32
+U8 = mybir.dt.uint8
+FP8X4 = mybir.dt.float8_e4m3fn_x4
+
+P = 128
+T_ROWS, D, E = 1024, 6144, 768
+N_PASS = 12
+FLOPS = 2 * T_ROWS * D * E
+NR = 7
+NX = 3
+
+
+def tile_longcatrouter_kernel(tc, hidden_states, weight, out):
+    nc = tc.nc
+    hid = hidden_states.rearrange("(i p) k -> p i k", p=P)
+    wgt = weight.rearrange("(a p) k -> p a k", p=P)
+
+    with ExitStack() as ctx:
+        const = ctx.enter_context(tc.tile_pool(name="const", bufs=1))
+        keep = ctx.enter_context(tc.tile_pool(name="keep", bufs=1))
+        rawp = ctx.enter_context(tc.tile_pool(name="rawp", bufs=NR))
+        xp = ctx.enter_context(tc.tile_pool(name="xp", bufs=NX))
+        grp = ctx.enter_context(tc.tile_pool(name="grp", bufs=6))
+        osp = ctx.enter_context(tc.tile_pool(name="osp", bufs=4))
+        psum = ctx.enter_context(tc.psum_pool(name="psum", bufs=1))
+        ctx.enter_context(tc.manual_schedule())
+
+        raw = {}
+        st = {"next": 0, "raw_free": NR, "x_free": NX, "bank": 0}
+
+        def new_raw(kind, c):
+            if kind == "x":
+                t = xp.tile([P, 2 * 1024], BF16, name="xraw", tag="xraw")
+            else:
+                t = rawp.tile([P, 4 * 1024], BF16, name="raw", tag="raw")
+            raw[(kind, c)] = t
+            return t
+
+        def source(kind, k0, k1):
+            if kind == "w":
+                return wgt[:, 0:4, k0:k1]
+            if kind == "x":
+                return wgt[:, 4:6, k0:k1]
+            if kind == "h":
+                return hid[:, 0:4, k0:k1]
+            return hid[:, 4:8, k0:k1]
+
+        w0 = new_raw("w", 0)
+        h0 = new_raw("h", 0)
+        st["raw_free"] -= 2
+        for pl in range(2):
+            for kind, t in (("w", w0), ("h", h0)):
+                nc.sync.dma_start(
+                    out=t[:].rearrange("p (a k) -> p a k", a=4)[:, :, 512 * pl : 512 * (pl + 1)],
+                    in_=source(kind, 512 * pl, 512 * (pl + 1)),
+                )
+
+        loads = []
+        for c in range(1, 6):
+            loads.extend([("w", c), ("h", c)])
+        for c in range(6):
+            loads.extend([("g", c), ("x", c)])
+
+        def pump():
+            while st["next"] < len(loads):
+                kind, c = loads[st["next"]]
+                key = "x_free" if kind == "x" else "raw_free"
+                if st[key] == 0:
+                    break
+                st[key] -= 1
+                st["next"] += 1
+                t = new_raw(kind, c)
+                na = 2 if kind == "x" else 4
+                nc.sync.dma_start(
+                    out=t[:].rearrange("p (a k) -> p a k", a=na),
+                    in_=source(kind, 1024 * c, 1024 * (c + 1)),
+                )
+
+        pump()
+
+        ident = const.tile([P, P], F32)
+        make_identity(nc, ident[:])
+
+        cA = keep.tile([P, N_PASS * 1024], U32, align_bytes=64)
+        sA = keep.tile([P, N_PASS * 1024], U8, align_bytes=64)
+        cH = keep.tile([P, N_PASS * 512], U32, align_bytes=64)
+        sH = keep.tile([P, N_PASS * 512], U8, align_bytes=64)
+        cX = keep.tile([P, N_PASS * 256], U32, align_bytes=64)
+        sX = keep.tile([P, N_PASS * 256], U8, align_bytes=64)
+
+        def bank(words, offs, on_vector, gt, half):
+            b = st["bank"]
+            st["bank"] = (b + 1) % 4
+            bk = psum.tile([P, 512], F32, name="tb%d" % b, tag="tb%d" % b)
+            for a in range(2):
+                for u in range(2):
+                    j = 2 * a + u
+                    nc.tensor.transpose(
+                        bk[:, 128 * j : 128 * (j + 1)],
+                        words[:, offs[a] + 128 * u : offs[a] + 128 * (u + 1)],
+                        ident[:],
+                    )
+            dst = gt[:].bitcast(F32)[:, 512 * half : 512 * (half + 1)].rearrange(
+                "p (a r u) -> p a r u", a=2, u=2
+            )
+            src = bk[:].rearrange("p (a u r) -> p a r u", a=2, u=2)
+            if on_vector:
+                nc.vector.tensor_copy(out=dst, in_=src)
+            else:
+                nc.scalar.copy(out=dst, in_=src)
+
+        def new_group():
+            gt = grp.tile([P, 2048], BF16, name="grouped", tag="grouped", align_bytes=64)
+            return gt
+
+        def quant(gt, codes, scales, c0):
+            nc.vector.quantize_mx(
+                out=codes[:, c0 : c0 + 512].bitcast(FP8X4),
+                scales=scales[:, c0 : c0 + 512],
+                in_=gt[:],
+            )
+
+        def t_four(kind, c, pl, eng):
+            words = raw[(kind, c)][:].bitcast(F32)
+            gt = new_group()
+            bank(words, (256 * pl, 512 + 256 * pl), eng[0], gt, 0)
+            bank(words, (1024 + 256 * pl, 1536 + 256 * pl), eng[1], gt, 1)
+            return gt
+
+        def dest(kind, g):
+            if kind == "w":
+                return (cA, sA, 1024 * g)
+            if kind == "h":
+                return (cA, sA, 1024 * g + 512)
+            return (cH, sH, 512 * g)
+
+        def t8(kind, c, pl):
+            gt = t_four(kind, c, pl, (False, True))
+            quant(gt, *dest(kind, 2 * c + pl))
+
+        def t16(kind, c):
+            g0 = t_four(kind, c, 0, (False, False))
+            g1 = t_four(kind, c, 1, (False, True))
+            quant(g0, *dest(kind, 2 * c))
+            quant(g1, *dest(kind, 2 * c + 1))
+            st["raw_free"] += 1
+            pump()
+
+        def t24(q):
+            words = raw[("g", q)][:].bitcast(F32)
+            xw = raw[("x", q)][:].bitcast(F32)
+            g0 = new_group()
+            bank(words, (0, 512), False, g0, 0)
+            bank(words, (1024, 1536), False, g0, 1)
+            g1 = new_group()
+            bank(words, (256, 768), True, g1, 0)
+            quant(g0, cH, sH, 512 * (2 * q))
+            bank(words, (1280, 1792), False, g1, 1)
+            g2 = new_group()
+            bank(xw, (0, 512), False, g2, 0)
+            bank(xw, (256, 768), True, g2, 1)
+            quant(g1, cH, sH, 512 * (2 * q + 1))
+            quant(g2, cX, sX, 512 * q)
+            st["raw_free"] += 1
+            st["x_free"] += 1
+            pump()
+
+        def mx(acc_ap, lc, ls, l0, rc, rs, r0, n, start, stop):
+            nc.tensor.matmul_mx(
+                out=acc_ap,
+                lhsT=lc[:, l0 : l0 + P].bitcast(FP8X4),
+                lhsT_scale=ls[:, l0 : l0 + P],
+                rhs=rc[:, r0 : r0 + n].bitcast(FP8X4),
+                rhs_scale=rs[:, r0 : r0 + n],
+                start=start,
+                stop=stop,
+            )
+
+        acc = {}
+
+        def open_acc():
+            for i in range(4):
+                acc[i] = psum.tile([P, 512], F32, name="acc%d" % i, tag="acc%d" % i)
+
+        def drain_acc(first_tile):
+            for i in range(4):
+                ot = osp.tile([P, 512], F32, name="ost", tag="ost")
+                if i % 2 == 0:
+                    nc.vector.tensor_copy(out=ot[:], in_=acc[i][:])
+                else:
+                    nc.scalar.copy(out=ot[:], in_=acc[i][:])
+                r0 = P * (first_tile + i)
+                nc.sync.dma_start(out=out[r0 : r0 + P, 0:512], in_=ot[:])
+
+        def m_first(g):
+            if g == 0:
+                open_acc()
+            for i in range(4):
+                mx(acc[i][:], cA, sA, 1024 * g + 512 + P * i, cA, sA, 1024 * g, 512,
+                   g == 0, g == N_PASS - 1)
+            if g == N_PASS - 1:
+                drain_acc(0)
+
+        def m_second(q):
+            if q == 0:
+                open_acc()
+            for g in (2 * q, 2 * q + 1):
+                for i in range(4):
+                    mx(acc[i][:], cH, sH, 512 * g + P * i, cA, sA, 1024 * g, 512,
+                       g == 0, g == N_PASS - 1)
+            if q == 5:
+                drain_acc(4)
+
+        t8("w", 0, 0)
+        t8("h", 0, 0)
+        t8("w", 0, 1)
+        m_first(0)
+        t8("h", 0, 1)
+        st["raw_free"] += 2
+        pump()
+        t16("w", 1)
+        m_first(1)
+        t16("h", 1)
+        for c in range(2, 6):
+            t16("w", c)
+            m_first(2 * c - 2)
+            t16("h", c)
+            m_first(2 * c - 1)
+
+        t24(0)
+        m_first(10)
+        t24(1)
+        m_first(11)
+        for q in range(2, 6):
+            t24(q)
+            m_second(q - 2)
+        m_second(4)
+        m_second(5)
+
+        tags = ["tb0", "tb1", "tb2", "tb3", "acc0", "acc1", "acc2", "acc3"]
+        for i in range(8):
+            pt = psum.tile([P, 512], F32, name="r3_%d" % i, tag=tags[i])
+            for g in range(N_PASS):
+                if i < 4:
+                    mx(pt[:, 0:256], cA, sA, 1024 * g + 512 + P * i, cX, sX, 256 * g, 256,
+                       g == 0, g == N_PASS - 1)
+                else:
+                    mx(pt[:, 0:256], cH, sH, 512 * g + P * (i - 4), cX, sX, 256 * g, 256,
+                       g == 0, g == N_PASS - 1)
+            o3 = osp.tile([P, 256], F32, name="o3", tag="o3")
+            if i % 2 == 0:
+                nc.vector.tensor_copy(out=o3[:], in_=pt[:, 0:256])
+            else:
+                nc.scalar.copy(out=o3[:], in_=pt[:, 0:256])
+            nc.sync.dma_start(out=out[P * i : P * (i + 1), 512:768], in_=o3[:])

@@ -14,7 +14,7 @@ T_ROWS, D, E = 1024, 6144, 768
 N_PASS = 12
 FLOPS = 2 * T_ROWS * D * E
 NR = 7
-NX = 3
+NX = 4
 
 
 def tile_longcatrouter_kernel(tc, hidden_states, weight, out):
@@ -27,7 +27,7 @@ def tile_longcatrouter_kernel(tc, hidden_states, weight, out):
         keep = ctx.enter_context(tc.tile_pool(name="keep", bufs=1))
         rawp = ctx.enter_context(tc.tile_pool(name="rawp", bufs=NR))
         xp = ctx.enter_context(tc.tile_pool(name="xp", bufs=NX))
-        grp = ctx.enter_context(tc.tile_pool(name="grp", bufs=6))
+        grp = ctx.enter_context(tc.tile_pool(name="grp", bufs=8))
         osp = ctx.enter_context(tc.tile_pool(name="osp", bufs=4))
         psum = ctx.enter_context(tc.psum_pool(name="psum", bufs=1))
         ctx.enter_context(tc.manual_schedule())
@@ -153,6 +153,18 @@ def tile_longcatrouter_kernel(tc, hidden_states, weight, out):
             st["raw_free"] += 1
             pump()
 
+        def t32(c):
+            gw0 = t_four("w", c, 0, (False, True))
+            gw1 = t_four("w", c, 1, (False, False))
+            quant(gw0, *dest("w", 2 * c))
+            gh0 = t_four("h", c, 0, (True, False))
+            gh1 = t_four("h", c, 1, (True, False))
+            quant(gw1, *dest("w", 2 * c + 1))
+            quant(gh0, *dest("h", 2 * c))
+            quant(gh1, *dest("h", 2 * c + 1))
+            st["raw_free"] += 2
+            pump()
+
         def t24(q):
             words = raw[("g", q)][:].bitcast(F32)
             xw = raw[("x", q)][:].bitcast(F32)
@@ -229,20 +241,22 @@ def tile_longcatrouter_kernel(tc, hidden_states, weight, out):
         m_first(1)
         t16("h", 1)
         for c in range(2, 6):
-            t16("w", c)
+            t32(c)
             m_first(2 * c - 2)
-            t16("h", c)
             m_first(2 * c - 1)
 
         t24(0)
         m_first(10)
         t24(1)
         m_first(11)
+        t24(2)
+        t24(3)
+        m_second(0)
+        m_second(1)
+        t24(4)
+        t24(5)
         for q in range(2, 6):
-            t24(q)
-            m_second(q - 2)
-        m_second(4)
-        m_second(5)
+            m_second(q)
 
         tags = ["tb0", "tb1", "tb2", "tb3", "acc0", "acc1", "acc2", "acc3"]
         for i in range(8):

@@ -13,8 +13,7 @@ P = 128
 T_ROWS, D, E = 1024, 6144, 768
 N_PASS = 12
 FLOPS = 2 * T_ROWS * D * E
-NR = 7
-NX = 4
+NR = 6
 
 
 def tile_longcatrouter_kernel(tc, hidden_states, weight, out):
@@ -26,31 +25,24 @@ def tile_longcatrouter_kernel(tc, hidden_states, weight, out):
         const = ctx.enter_context(tc.tile_pool(name="const", bufs=1))
         keep = ctx.enter_context(tc.tile_pool(name="keep", bufs=1))
         rawp = ctx.enter_context(tc.tile_pool(name="rawp", bufs=NR))
-        xp = ctx.enter_context(tc.tile_pool(name="xp", bufs=NX))
-        grp = ctx.enter_context(tc.tile_pool(name="grp", bufs=8))
+        grp = ctx.enter_context(tc.tile_pool(name="grp", bufs=6))
         osp = ctx.enter_context(tc.tile_pool(name="osp", bufs=4))
         psum = ctx.enter_context(tc.psum_pool(name="psum", bufs=1))
         ctx.enter_context(tc.manual_schedule())
 
         raw = {}
-        st = {"next": 0, "raw_free": NR, "x_free": NX, "bank": 0}
+        st = {"next": 0, "raw_free": NR, "bank": 0}
 
         def new_raw(kind, c):
-            if kind == "x":
-                t = xp.tile([P, 2 * 1024], BF16, name="xraw", tag="xraw")
-            else:
-                t = rawp.tile([P, 4 * 1024], BF16, name="raw", tag="raw")
+            width = 4096 if kind in ("w", "h") else 6144
+            t = rawp.tile([P, width], BF16, name="raw", tag="raw")
             raw[(kind, c)] = t
             return t
 
         def source(kind, k0, k1):
             if kind == "w":
                 return wgt[:, 0:4, k0:k1]
-            if kind == "x":
-                return wgt[:, 4:6, k0:k1]
-            if kind == "h":
-                return hid[:, 0:4, k0:k1]
-            return hid[:, 4:8, k0:k1]
+            return hid[:, 0:4, k0:k1]
 
         w0 = new_raw("w", 0)
         h0 = new_raw("h", 0)
@@ -65,23 +57,28 @@ def tile_longcatrouter_kernel(tc, hidden_states, weight, out):
         loads = []
         for c in range(1, 6):
             loads.extend([("w", c), ("h", c)])
-        for c in range(6):
-            loads.extend([("g", c), ("x", c)])
+        loads.extend([("x", 0), ("x", 1), ("g", 4), ("g", 5), ("g", 6), ("g", 7)])
 
         def pump():
             while st["next"] < len(loads):
                 kind, c = loads[st["next"]]
-                key = "x_free" if kind == "x" else "raw_free"
-                if st[key] == 0:
+                if st["raw_free"] == 0:
                     break
-                st[key] -= 1
+                st["raw_free"] -= 1
                 st["next"] += 1
                 t = new_raw(kind, c)
-                na = 2 if kind == "x" else 4
-                nc.sync.dma_start(
-                    out=t[:].rearrange("p (a k) -> p a k", a=na),
-                    in_=source(kind, 1024 * c, 1024 * (c + 1)),
-                )
+                if kind == "x":
+                    nc.sync.dma_start(
+                        out=t[:].rearrange("p (a k) -> p a k", a=2),
+                        in_=wgt[:, 4:6, 3072 * c : 3072 * (c + 1)],
+                    )
+                elif kind == "g":
+                    nc.sync.dma_start(out=t[:], in_=hid[:, c, :])
+                else:
+                    nc.sync.dma_start(
+                        out=t[:].rearrange("p (a k) -> p a k", a=4),
+                        in_=source(kind, 1024 * c, 1024 * (c + 1)),
+                    )
 
         pump()
 
@@ -137,9 +134,7 @@ def tile_longcatrouter_kernel(tc, hidden_states, weight, out):
         def dest(kind, g):
             if kind == "w":
                 return (cA, sA, 1024 * g)
-            if kind == "h":
-                return (cA, sA, 1024 * g + 512)
-            return (cH, sH, 512 * g)
+            return (cA, sA, 1024 * g + 512)
 
         def t8(kind, c, pl):
             gt = t_four(kind, c, pl, (False, True))
@@ -153,36 +148,31 @@ def tile_longcatrouter_kernel(tc, hidden_states, weight, out):
             st["raw_free"] += 1
             pump()
 
-        def t32(c):
-            gw0 = t_four("w", c, 0, (False, True))
-            gw1 = t_four("w", c, 1, (False, False))
-            quant(gw0, *dest("w", 2 * c))
-            gh0 = t_four("h", c, 0, (True, False))
-            gh1 = t_four("h", c, 1, (True, False))
-            quant(gw1, *dest("w", 2 * c + 1))
-            quant(gh0, *dest("h", 2 * c))
-            quant(gh1, *dest("h", 2 * c + 1))
-            st["raw_free"] += 2
+        def t24(words, offs, codes, scales, c0):
+            g0 = new_group()
+            bank(words, offs[0], False, g0, 0)
+            bank(words, offs[1], False, g0, 1)
+            g1 = new_group()
+            bank(words, offs[2], True, g1, 0)
+            quant(g0, codes, scales, c0[0])
+            bank(words, offs[3], False, g1, 1)
+            g2 = new_group()
+            bank(words, offs[4], False, g2, 0)
+            bank(words, offs[5], True, g2, 1)
+            quant(g1, codes, scales, c0[1])
+            quant(g2, codes, scales, c0[2])
+            st["raw_free"] += 1
             pump()
 
-        def t24(q):
-            words = raw[("g", q)][:].bitcast(F32)
-            xw = raw[("x", q)][:].bitcast(F32)
-            g0 = new_group()
-            bank(words, (0, 512), False, g0, 0)
-            bank(words, (1024, 1536), False, g0, 1)
-            g1 = new_group()
-            bank(words, (256, 768), True, g1, 0)
-            quant(g0, cH, sH, 512 * (2 * q))
-            bank(words, (1280, 1792), False, g1, 1)
-            g2 = new_group()
-            bank(xw, (0, 512), False, g2, 0)
-            bank(xw, (256, 768), True, g2, 1)
-            quant(g1, cH, sH, 512 * (2 * q + 1))
-            quant(g2, cX, sX, 512 * q)
-            st["raw_free"] += 1
-            st["x_free"] += 1
-            pump()
+        def tx(half):
+            words = raw[("x", half)][:].bitcast(F32)
+            offs = [(256 * pl, 1536 + 256 * pl) for pl in range(6)]
+            t24(words, offs, cX, sX, [256 * (6 * half + 2 * q) for q in range(3)])
+
+        def tg(i):
+            words = raw[("g", i)][:].bitcast(F32)
+            offs = [(256 * (2 * b), 256 * (2 * b + 1)) for b in range(6)]
+            t24(words, offs, cH, sH, [1536 * (i - 4) + 512 * m for m in range(3)])
 
         def mx(acc_ap, lc, ls, l0, rc, rs, r0, n, start, stop):
             nc.tensor.matmul_mx(
@@ -220,15 +210,39 @@ def tile_longcatrouter_kernel(tc, hidden_states, weight, out):
             if g == N_PASS - 1:
                 drain_acc(0)
 
-        def m_second(q):
-            if q == 0:
+        def store_small(src_ap, i, on_vector):
+            o3 = osp.tile([P, 256], F32, name="o3", tag="o3")
+            if on_vector:
+                nc.vector.tensor_copy(out=o3[:], in_=src_ap)
+            else:
+                nc.scalar.copy(out=o3[:], in_=src_ap)
+            nc.sync.dma_start(out=out[P * i : P * (i + 1), 512:768], in_=o3[:])
+
+        def r3a(half):
+            if half == 0:
                 open_acc()
-            for g in (2 * q, 2 * q + 1):
+            for g in range(6 * half, 6 * half + 6):
                 for i in range(4):
-                    mx(acc[i][:], cH, sH, 512 * g + P * i, cA, sA, 1024 * g, 512,
+                    mx(acc[i][:, 0:256], cA, sA, 1024 * g + 512 + P * i, cX, sX, 256 * g, 256,
                        g == 0, g == N_PASS - 1)
-            if q == 5:
-                drain_acc(4)
+            if half == 1:
+                for i in range(4):
+                    store_small(acc[i][:, 0:256], i, i % 2 == 0)
+
+        def mc(i):
+            j = 2 * (i % 2)
+            pa = psum.tile([P, 512], F32, name="mca%d" % i, tag="acc%d" % j)
+            pb = psum.tile([P, 512], F32, name="mcb%d" % i, tag="acc%d" % (j + 1))
+            for g in range(N_PASS):
+                mx(pa[:], cH, sH, 1536 * (i - 4) + P * g, cA, sA, 1024 * g, 512,
+                   g == 0, g == N_PASS - 1)
+            ot = osp.tile([P, 512], F32, name="ost", tag="ost")
+            nc.vector.tensor_copy(out=ot[:], in_=pa[:])
+            nc.sync.dma_start(out=out[P * i : P * (i + 1), 0:512], in_=ot[:])
+            for g in range(N_PASS):
+                mx(pb[:, 0:256], cH, sH, 1536 * (i - 4) + P * g, cX, sX, 256 * g, 256,
+                   g == 0, g == N_PASS - 1)
+            store_small(pb[:, 0:256], i, False)
 
         t8("w", 0, 0)
         t8("h", 0, 0)
@@ -241,36 +255,22 @@ def tile_longcatrouter_kernel(tc, hidden_states, weight, out):
         m_first(1)
         t16("h", 1)
         for c in range(2, 6):
-            t32(c)
+            t16("w", c)
             m_first(2 * c - 2)
+            t16("h", c)
             m_first(2 * c - 1)
 
-        t24(0)
+        tx(0)
         m_first(10)
-        t24(1)
+        tx(1)
         m_first(11)
-        t24(2)
-        t24(3)
-        m_second(0)
-        m_second(1)
-        t24(4)
-        t24(5)
-        for q in range(2, 6):
-            m_second(q)
-
-        tags = ["tb0", "tb1", "tb2", "tb3", "acc0", "acc1", "acc2", "acc3"]
-        for i in range(8):
-            pt = psum.tile([P, 512], F32, name="r3_%d" % i, tag=tags[i])
-            for g in range(N_PASS):
-                if i < 4:
-                    mx(pt[:, 0:256], cA, sA, 1024 * g + 512 + P * i, cX, sX, 256 * g, 256,
-                       g == 0, g == N_PASS - 1)
-                else:
-                    mx(pt[:, 0:256], cH, sH, 512 * g + P * (i - 4), cX, sX, 256 * g, 256,
-                       g == 0, g == N_PASS - 1)
-            o3 = osp.tile([P, 256], F32, name="o3", tag="o3")
-            if i % 2 == 0:
-                nc.vector.tensor_copy(out=o3[:], in_=pt[:, 0:256])
-            else:
-                nc.scalar.copy(out=o3[:], in_=pt[:, 0:256])
-            nc.sync.dma_start(out=out[P * i : P * (i + 1), 512:768], in_=o3[:])
+        tg(4)
+        r3a(0)
+        tg(5)
+        r3a(1)
+        tg(6)
+        mc(4)
+        tg(7)
+        mc(5)
+        mc(6)
+        mc(7)

@@ -20,6 +20,7 @@ def tile_longcatrouter_kernel(tc, hidden_states, weight, out):
     nc = tc.nc
     hid = hidden_states.rearrange("(i p) k -> p i k", p=P)
     wgt = weight.rearrange("(a p) k -> p a k", p=P)
+    hv = hidden_states.rearrange("t (g q) -> (t g) q", q=512)
 
     with ExitStack() as ctx:
         const = ctx.enter_context(tc.tile_pool(name="const", bufs=1))
@@ -35,7 +36,7 @@ def tile_longcatrouter_kernel(tc, hidden_states, weight, out):
 
         def new_raw(kind, c):
             width = 4096 if kind in ("w", "h") else 6144
-            t = rawp.tile([P, width], BF16, name="raw", tag="raw")
+            t = rawp.tile([P, width], BF16, name="raw", tag="raw", align_bytes=64)
             raw[(kind, c)] = t
             return t
 
@@ -57,7 +58,7 @@ def tile_longcatrouter_kernel(tc, hidden_states, weight, out):
         loads = []
         for c in range(1, 6):
             loads.extend([("w", c), ("h", c)])
-        loads.extend([("x", 0), ("x", 1), ("g", 4), ("g", 5), ("g", 6), ("g", 7)])
+        loads.extend([("x", 0), ("x", 1), ("g", 4), ("g", 5)])
 
         def pump():
             while st["next"] < len(loads):
@@ -174,6 +175,43 @@ def tile_longcatrouter_kernel(tc, hidden_states, weight, out):
             offs = [(256 * (2 * b), 256 * (2 * b + 1)) for b in range(6)]
             t24(words, offs, cH, sH, [1536 * (i - 4) + 512 * m for m in range(3)])
 
+        def load_v(i):
+            t = new_raw("v", i)
+            rows = hv[1536 * i : 1536 * (i + 1), :].rearrange("(c s) q -> c s q", s=96)
+            for hb in range(2):
+                for a in range(4):
+                    for u in range(2):
+                        k0 = 256 * u + 64 * a
+                        nc.sync.dma_start(
+                            out=t[32 * a + u : 32 * a + 32 : 2, 3072 * hb : 3072 * (hb + 1)].rearrange(
+                                "p (s q) -> p s q", q=64
+                            ),
+                            in_=rows[:, 48 * hb : 48 * (hb + 1), k0 : k0 + 64],
+                        )
+
+        def vt(i):
+            words = raw[("v", i)][:].bitcast(F32)
+            groups = [new_group(), new_group(), new_group()]
+
+            def block(m, hb):
+                gw = groups[m][:].bitcast(F32)
+                for gl in range(4):
+                    g = 4 * m + gl
+                    for b in range(4 * hb, 4 * hb + 4):
+                        nc.vector.transpose(
+                            out=gw[:, 256 * gl + 32 * b : 256 * gl + 32 * (b + 1)],
+                            in_=words[:, 32 * (12 * b + g) : 32 * (12 * b + g + 1)],
+                        )
+
+            for m in range(3):
+                block(m, 0)
+            block(0, 1)
+            block(1, 1)
+            quant(groups[0], cH, sH, 1536 * (i - 4))
+            block(2, 1)
+            quant(groups[1], cH, sH, 1536 * (i - 4) + 512)
+            quant(groups[2], cH, sH, 1536 * (i - 4) + 1024)
+
         def mx(acc_ap, lc, ls, l0, rc, rs, r0, n, start, stop):
             nc.tensor.matmul_mx(
                 out=acc_ap,
@@ -210,13 +248,22 @@ def tile_longcatrouter_kernel(tc, hidden_states, weight, out):
             if g == N_PASS - 1:
                 drain_acc(0)
 
-        def store_small(src_ap, i, on_vector):
-            o3 = osp.tile([P, 256], F32, name="o3", tag="o3")
-            if on_vector:
-                nc.vector.tensor_copy(out=o3[:], in_=src_ap)
+        def out_rows(i, c0, c1):
+            rows = out[P * i : P * (i + 1), c0:c1]
+            if i >= 6:
+                return rows.rearrange("(c b) n -> b c n", b=8)
+            return rows
+
+        def store(src_ap, i, c0, c1):
+            if c1 - c0 == 256:
+                ot = osp.tile([P, 256], F32, name="o3", tag="o3")
             else:
-                nc.scalar.copy(out=o3[:], in_=src_ap)
-            nc.sync.dma_start(out=out[P * i : P * (i + 1), 512:768], in_=o3[:])
+                ot = osp.tile([P, 512], F32, name="ost", tag="ost")
+            nc.scalar.copy(out=ot[:], in_=src_ap)
+            if i == 7:
+                nc.sync.dma_start(out=out_rows(i, c0, c1), in_=ot[:])
+            else:
+                nc.scalar.dma_start(out=out_rows(i, c0, c1), in_=ot[:])
 
         def r3a(half):
             if half == 0:
@@ -227,7 +274,7 @@ def tile_longcatrouter_kernel(tc, hidden_states, weight, out):
                        g == 0, g == N_PASS - 1)
             if half == 1:
                 for i in range(4):
-                    store_small(acc[i][:, 0:256], i, i % 2 == 0)
+                    store(acc[i][:, 0:256], i, 512, 768)
 
         def mc(i):
             j = 2 * (i % 2)
@@ -236,13 +283,11 @@ def tile_longcatrouter_kernel(tc, hidden_states, weight, out):
             for g in range(N_PASS):
                 mx(pa[:], cH, sH, 1536 * (i - 4) + P * g, cA, sA, 1024 * g, 512,
                    g == 0, g == N_PASS - 1)
-            ot = osp.tile([P, 512], F32, name="ost", tag="ost")
-            nc.vector.tensor_copy(out=ot[:], in_=pa[:])
-            nc.sync.dma_start(out=out[P * i : P * (i + 1), 0:512], in_=ot[:])
+            store(pa[:], i, 0, 512)
             for g in range(N_PASS):
                 mx(pb[:, 0:256], cH, sH, 1536 * (i - 4) + P * g, cX, sX, 256 * g, 256,
                    g == 0, g == N_PASS - 1)
-            store_small(pb[:, 0:256], i, False)
+            store(pb[:, 0:256], i, 512, 768)
 
         t8("w", 0, 0)
         t8("h", 0, 0)
@@ -264,13 +309,15 @@ def tile_longcatrouter_kernel(tc, hidden_states, weight, out):
         m_first(10)
         tx(1)
         m_first(11)
+        load_v(6)
+        load_v(7)
         tg(4)
         r3a(0)
         tg(5)
         r3a(1)
-        tg(6)
+        vt(6)
         mc(4)
-        tg(7)
+        vt(7)
         mc(5)
         mc(6)
         mc(7)

from contextlib import ExitStack

import concourse.mybir as mybir
from concourse.masks import make_identity

F32 = mybir.dt.float32
BF16 = mybir.dt.bfloat16
U32 = mybir.dt.uint32
U8 = mybir.dt.uint8
FP8X4 = mybir.dt.float8_e4m3fn_x4

P = 128
T_ROWS, D, E = 1024, 6144, 768
N_PASS = 12
FLOPS = 2 * T_ROWS * D * E
NR = 6


def tile_longcatrouter_kernel(tc, hidden_states, weight, out):
    nc = tc.nc
    hid = hidden_states.rearrange("(i p) k -> p i k", p=P)
    wgt = weight.rearrange("(a p) k -> p a k", p=P)
    hv = hidden_states.rearrange("t (g q) -> (t g) q", q=512)

    with ExitStack() as ctx:
        const = ctx.enter_context(tc.tile_pool(name="const", bufs=1))
        keep = ctx.enter_context(tc.tile_pool(name="keep", bufs=1))
        rawp = ctx.enter_context(tc.tile_pool(name="rawp", bufs=NR))
        grp = ctx.enter_context(tc.tile_pool(name="grp", bufs=6))
        osp = ctx.enter_context(tc.tile_pool(name="osp", bufs=4))
        psum = ctx.enter_context(tc.psum_pool(name="psum", bufs=1))
        ctx.enter_context(tc.manual_schedule())

        raw = {}
        st = {"next": 0, "raw_free": NR, "bank": 0}

        def new_raw(kind, c):
            width = 4096 if kind in ("w", "h") else 6144
            t = rawp.tile([P, width], BF16, name="raw", tag="raw", align_bytes=64)
            raw[(kind, c)] = t
            return t

        def source(kind, k0, k1):
            if kind == "w":
                return wgt[:, 0:4, k0:k1]
            return hid[:, 0:4, k0:k1]

        w0 = new_raw("w", 0)
        h0 = new_raw("h", 0)
        st["raw_free"] -= 2
        for pl in range(2):
            for kind, t in (("w", w0), ("h", h0)):
                nc.sync.dma_start(
                    out=t[:].rearrange("p (a k) -> p a k", a=4)[:, :, 512 * pl : 512 * (pl + 1)],
                    in_=source(kind, 512 * pl, 512 * (pl + 1)),
                )

        loads = []
        for c in range(1, 6):
            loads.extend([("w", c), ("h", c)])
        loads.extend([("x", 0), ("x", 1), ("g", 4), ("g", 5)])

        def pump():
            while st["next"] < len(loads):
                kind, c = loads[st["next"]]
                if st["raw_free"] == 0:
                    break
                st["raw_free"] -= 1
                st["next"] += 1
                t = new_raw(kind, c)
                if kind == "x":
                    nc.sync.dma_start(
                        out=t[:].rearrange("p (a k) -> p a k", a=2),
                        in_=wgt[:, 4:6, 3072 * c : 3072 * (c + 1)],
                    )
                elif kind == "g":
                    nc.sync.dma_start(out=t[:], in_=hid[:, c, :])
                else:
                    nc.sync.dma_start(
                        out=t[:].rearrange("p (a k) -> p a k", a=4),
                        in_=source(kind, 1024 * c, 1024 * (c + 1)),
                    )

        pump()

        ident = const.tile([P, P], F32)
        make_identity(nc, ident[:])

        cA = keep.tile([P, N_PASS * 1024], U32, align_bytes=64)
        sA = keep.tile([P, N_PASS * 1024], U8, align_bytes=64)
        cH = keep.tile([P, N_PASS * 512], U32, align_bytes=64)
        sH = keep.tile([P, N_PASS * 512], U8, align_bytes=64)
        cX = keep.tile([P, N_PASS * 256], U32, align_bytes=64)
        sX = keep.tile([P, N_PASS * 256], U8, align_bytes=64)

        def bank(words, offs, on_vector, gt, half):
            b = st["bank"]
            st["bank"] = (b + 1) % 4
            bk = psum.tile([P, 512], F32, name="tb%d" % b, tag="tb%d" % b)
            for a in range(2):
                for u in range(2):
                    j = 2 * a + u
                    nc.tensor.transpose(
                        bk[:, 128 * j : 128 * (j + 1)],
                        words[:, offs[a] + 128 * u : offs[a] + 128 * (u + 1)],
                        ident[:],
                    )
            dst = gt[:].bitcast(F32)[:, 512 * half : 512 * (half + 1)].rearrange(
                "p (a r u) -> p a r u", a=2, u=2
            )
            src = bk[:].rearrange("p (a u r) -> p a r u", a=2, u=2)
            if on_vector:
                nc.vector.tensor_copy(out=dst, in_=src)
            else:
                nc.scalar.copy(out=dst, in_=src)

        def new_group():
            gt = grp.tile([P, 2048], BF16, name="grouped", tag="grouped", align_bytes=64)
            return gt

        def quant(gt, codes, scales, c0):
            nc.vector.quantize_mx(
                out=codes[:, c0 : c0 + 512].bitcast(FP8X4),
                scales=scales[:, c0 : c0 + 512],
                in_=gt[:],
            )

        def t_four(kind, c, pl, eng):
            words = raw[(kind, c)][:].bitcast(F32)
            gt = new_group()
            bank(words, (256 * pl, 512 + 256 * pl), eng[0], gt, 0)
            bank(words, (1024 + 256 * pl, 1536 + 256 * pl), eng[1], gt, 1)
            return gt

        def dest(kind, g):
            if kind == "w":
                return (cA, sA, 1024 * g)
            return (cA, sA, 1024 * g + 512)

        def t8(kind, c, pl):
            gt = t_four(kind, c, pl, (False, True))
            quant(gt, *dest(kind, 2 * c + pl))

        def t16(kind, c):
            g0 = t_four(kind, c, 0, (False, False))
            g1 = t_four(kind, c, 1, (False, True))
            quant(g0, *dest(kind, 2 * c))
            quant(g1, *dest(kind, 2 * c + 1))
            st["raw_free"] += 1
            pump()

        def t24(words, offs, codes, scales, c0):
            g0 = new_group()
            bank(words, offs[0], False, g0, 0)
            bank(words, offs[1], False, g0, 1)
            g1 = new_group()
            bank(words, offs[2], True, g1, 0)
            quant(g0, codes, scales, c0[0])
            bank(words, offs[3], False, g1, 1)
            g2 = new_group()
            bank(words, offs[4], False, g2, 0)
            bank(words, offs[5], True, g2, 1)
            quant(g1, codes, scales, c0[1])
            quant(g2, codes, scales, c0[2])
            st["raw_free"] += 1
            pump()

        def tx(half):
            words = raw[("x", half)][:].bitcast(F32)
            offs = [(256 * pl, 1536 + 256 * pl) for pl in range(6)]
            t24(words, offs, cX, sX, [256 * (6 * half + 2 * q) for q in range(3)])

        def tg(i):
            words = raw[("g", i)][:].bitcast(F32)
            offs = [(256 * (2 * b), 256 * (2 * b + 1)) for b in range(6)]
            t24(words, offs, cH, sH, [1536 * (i - 4) + 512 * m for m in range(3)])

        def load_v(i):
            t = new_raw("v", i)
            rows = hv[1536 * i : 1536 * (i + 1), :].rearrange("(c s) q -> c s q", s=96)
            for hb in range(2):
                for a in range(4):
                    for u in range(2):
                        k0 = 256 * u + 64 * a
                        nc.sync.dma_start(
                            out=t[32 * a + u : 32 * a + 32 : 2, 3072 * hb : 3072 * (hb + 1)].rearrange(
                                "p (s q) -> p s q", q=64
                            ),
                            in_=rows[:, 48 * hb : 48 * (hb + 1), k0 : k0 + 64],
                        )

        def vt(i):
            words = raw[("v", i)][:].bitcast(F32)
            groups = [new_group(), new_group(), new_group()]

            def block(m, hb):
                gw = groups[m][:].bitcast(F32)
                for gl in range(4):
                    g = 4 * m + gl
                    for b in range(4 * hb, 4 * hb + 4):
                        nc.vector.transpose(
                            out=gw[:, 256 * gl + 32 * b : 256 * gl + 32 * (b + 1)],
                            in_=words[:, 32 * (12 * b + g) : 32 * (12 * b + g + 1)],
                        )

            for m in range(3):
                block(m, 0)
            block(0, 1)
            block(1, 1)
            quant(groups[0], cH, sH, 1536 * (i - 4))
            block(2, 1)
            quant(groups[1], cH, sH, 1536 * (i - 4) + 512)
            quant(groups[2], cH, sH, 1536 * (i - 4) + 1024)

        def mx(acc_ap, lc, ls, l0, rc, rs, r0, n, start, stop):
            nc.tensor.matmul_mx(
                out=acc_ap,
                lhsT=lc[:, l0 : l0 + P].bitcast(FP8X4),
                lhsT_scale=ls[:, l0 : l0 + P],
                rhs=rc[:, r0 : r0 + n].bitcast(FP8X4),
                rhs_scale=rs[:, r0 : r0 + n],
                start=start,
                stop=stop,
            )

        acc = {}

        def open_acc():
            for i in range(4):
                acc[i] = psum.tile([P, 512], F32, name="acc%d" % i, tag="acc%d" % i)

        def drain_acc(first_tile):
            for i in range(4):
                ot = osp.tile([P, 512], F32, name="ost", tag="ost")
                if i % 2 == 0:
                    nc.vector.tensor_copy(out=ot[:], in_=acc[i][:])
                else:
                    nc.scalar.copy(out=ot[:], in_=acc[i][:])
                r0 = P * (first_tile + i)
                nc.sync.dma_start(out=out[r0 : r0 + P, 0:512], in_=ot[:])

        def m_first(g):
            if g == 0:
                open_acc()
            for i in range(4):
                mx(acc[i][:], cA, sA, 1024 * g + 512 + P * i, cA, sA, 1024 * g, 512,
                   g == 0, g == N_PASS - 1)
            if g == N_PASS - 1:
                drain_acc(0)

        def out_rows(i, c0, c1):
            rows = out[P * i : P * (i + 1), c0:c1]
            if i >= 6:
                return rows.rearrange("(c b) n -> b c n", b=8)
            return rows

        def store(src_ap, i, c0, c1):
            if c1 - c0 == 256:
                ot = osp.tile([P, 256], F32, name="o3", tag="o3")
            else:
                ot = osp.tile([P, 512], F32, name="ost", tag="ost")
            nc.scalar.copy(out=ot[:], in_=src_ap)
            if i == 7:
                nc.sync.dma_start(out=out_rows(i, c0, c1), in_=ot[:])
            else:
                nc.scalar.dma_start(out=out_rows(i, c0, c1), in_=ot[:])

        def r3a(half):
            if half == 0:
                open_acc()
            for g in range(6 * half, 6 * half + 6):
                for i in range(4):
                    mx(acc[i][:, 0:256], cA, sA, 1024 * g + 512 + P * i, cX, sX, 256 * g, 256,
                       g == 0, g == N_PASS - 1)
            if half == 1:
                for i in range(4):
                    store(acc[i][:, 0:256], i, 512, 768)

        def mc(i):
            j = 2 * (i % 2)
            pa = psum.tile([P, 512], F32, name="mca%d" % i, tag="acc%d" % j)
            pb = psum.tile([P, 512], F32, name="mcb%d" % i, tag="acc%d" % (j + 1))
            for g in range(N_PASS):
                mx(pa[:], cH, sH, 1536 * (i - 4) + P * g, cA, sA, 1024 * g, 512,
                   g == 0, g == N_PASS - 1)
            store(pa[:], i, 0, 512)
            for g in range(N_PASS):
                mx(pb[:, 0:256], cH, sH, 1536 * (i - 4) + P * g, cX, sX, 256 * g, 256,
                   g == 0, g == N_PASS - 1)
            store(pb[:, 0:256], i, 512, 768)

        t8("w", 0, 0)
        t8("h", 0, 0)
        t8("w", 0, 1)
        m_first(0)
        t8("h", 0, 1)
        st["raw_free"] += 2
        pump()
        t16("w", 1)
        m_first(1)
        t16("h", 1)
        for c in range(2, 6):
            t16("w", c)
            m_first(2 * c - 2)
            t16("h", c)
            m_first(2 * c - 1)

        tx(0)
        m_first(10)
        tx(1)
        m_first(11)
        load_v(6)
        load_v(7)
        tg(4)
        r3a(0)
        tg(5)
        r3a(1)
        vt(6)
        mc(4)
        vt(7)
        mc(5)
        mc(6)
        mc(7)
